import numpy as np
import ml_dtypes


def mxq(x, axis, fmt="e4m3"):
    dtype, down = {"e4m3": (ml_dtypes.float8_e4m3fn, 7), "e5m2": (ml_dtypes.float8_e5m2, 14)}[fmt]
    v = np.moveaxis(np.asarray(x, np.float32).astype(ml_dtypes.bfloat16).astype(np.float64), axis, -1)
    blocks = v.reshape(v.shape[:-1] + (-1, 32))
    amax = np.abs(blocks).max(-1, keepdims=True)
    byte = np.maximum(np.where(amax > 0, np.frexp(amax)[1] - 1 + 127, 0) - down, 1)
    scale = np.exp2(byte - 127.0)
    codes = (blocks / scale).astype(np.float32).astype(dtype).astype(np.float64)
    return np.moveaxis((codes * scale).reshape(v.shape), -1, axis)


WIDE = False


def mx_kscale(k):
    if not WIDE:
        return np.ones(k)
    levels = np.array([10, -10, 5, -5, 0])
    a = np.random.permutation(np.resize(levels, k // 512 * 4)).reshape(k // 512, 4)
    idx = np.arange(k)
    return np.exp2(a[idx // 512, idx % 128 // 32])


BF16 = ml_dtypes.bfloat16


def bf(x):
    return np.asarray(x, np.float32).astype(BF16)


def f64(x):
    return np.asarray(x).astype(np.float64)


S, D, H, HD = 8192, 512, 4, 32
W = H * HD


def rotary(xq, xk, freqs):
    ll = freqs[:, :, 0:1]
    rr = freqs[:, :, 1:2]
    fl = np.concatenate([ll, ll], axis=-1).reshape(S, 1, HD)
    fr = np.concatenate([-rr, rr], axis=-1).reshape(S, 1, HD)
    xq_ = xq.reshape(S, H, HD // 2, 2).reshape(S, H, HD)
    xk_ = xk.reshape(S, H, HD // 2, 2).reshape(S, H, HD)
    return xq * fl + xq_ * fr, xk * fl + xk_ * fr


def setup_inputs():
    s = mx_kscale(D)
    c = 1.0 / np.sqrt(D)
    theta = 10000.0 ** (-np.arange(0, HD, 2) / HD)
    angles = np.arange(S)[:, None] * theta[None, :]
    return {"x": bf(np.random.standard_normal((S, D)) * s),
            "freqs": bf(np.stack([np.cos(angles), np.sin(angles)], axis=-1)),
            "wq": bf(np.random.standard_normal((W, D)) * c / s[None, :]),
            "wk": bf(np.random.standard_normal((W, D)) * c / s[None, :]),
            "wv": bf(np.random.standard_normal((W, D)) * c / s[None, :])}


def reference(x, freqs, wq, wk, wv):
    xm = mxq(f64(x), 1, "e4m3")
    xq = xm @ mxq(f64(wq), 1, "e4m3").T
    xk = xm @ mxq(f64(wk), 1, "e4m3").T
    xv = xm @ mxq(f64(wv), 1, "e4m3").T
    xq = xq.reshape(S, H, HD)
    xk = xk.reshape(S, H, HD)
    xv = xv.reshape(S, H, HD)
    xq, xk = rotary(xq, xk, f64(freqs))
    q = np.transpose(xq, (1, 0, 2))
    k = np.transpose(xk, (1, 0, 2))
    v = np.transpose(xv, (1, 0, 2))
    return q, k, v

@@ -1,0 +1,177 @@
+import concourse.mybir as mybir
+from concourse.masks import make_identity
+
+F32 = mybir.dt.float32
+BF16 = mybir.dt.bfloat16
+U32 = mybir.dt.uint32
+U8 = mybir.dt.uint8
+FP8X4 = mybir.dt.float8_e4m3fn_x4
+MULT = mybir.AluOpType.mult
+ADD = mybir.AluOpType.add
+
+P = 128
+S = 8192
+D = 512
+HEADS = 4
+HD = 32
+W = HEADS * HD
+PACK = 4
+HALVES = 2
+
+TILES = S // P
+BANK_TILES = 2
+ROUND = 4
+LOAD = 8
+STORE = 16
+ROUNDS = TILES // ROUND
+
+FLOPS = 2 * S * D * 3 * W
+
+
+def features_onto_partitions(nc, banks, identity, words, grouped, tiles):
+    grouped_words = grouped.bitcast(F32).rearrange("p (t r u) -> p t r u", r=P, u=HALVES)
+    for first in range(0, tiles, BANK_TILES):
+        count = min(BANK_TILES, tiles - first)
+        bank = banks.tile([P, BANK_TILES, HALVES, P], F32, name="transposed")
+        for t in range(count):
+            for u in range(HALVES):
+                column = ((first + t) * HALVES + u) * P
+                nc.tensor.transpose(bank[:, t, u, :], words[:, column : column + P], identity)
+        nc.scalar.copy(
+            out=grouped_words[:, first : first + count],
+            in_=bank[:, 0:count].rearrange("p t u r -> p t r u"),
+        )
+
+
+def tile_attention_pa_t_kernel(tc, x, freqs, wq, wk, wv, out_0, out_1, out_2):
+    nc = tc.nc
+    x_rows = x.rearrange("(p t) k -> p (t k)", t=TILES)
+    freqs_rows = freqs.rearrange("(p t) j c -> p (t j c)", t=TILES)
+    out_rows = [o.rearrange("h (p t) d -> p h t d", t=TILES) for o in (out_0, out_1, out_2)]
+
+    with tc.manual_schedule(), tc.tile_pool(name="keep", bufs=1) as keep, tc.tile_pool(
+        name="stage", bufs=3
+    ) as stage, tc.tile_pool(name="results", bufs=TILES // STORE) as results, tc.psum_pool(
+        name="banks", bufs=2
+    ) as banks, tc.psum_pool(name="qk_banks", bufs=4) as qk_banks, tc.psum_pool(
+        name="v_banks", bufs=2
+    ) as v_banks:
+        w_sb = keep.tile([P, 3 * D], BF16)
+        for i, w in enumerate((wq, wk, wv)):
+            nc.sync.dma_start(out=w_sb[:, i * D : (i + 1) * D], in_=w)
+        x_sb = []
+        freqs_sb = keep.tile([P, TILES * HD], BF16)
+        for c in range(TILES // LOAD):
+            x_part = keep.tile([P, LOAD * D], BF16, name="x%d" % c)
+            nc.sync.dma_start(out=x_part[:], in_=x_rows[:, c * LOAD * D : (c + 1) * LOAD * D])
+            x_sb.append(x_part)
+            if c == 0:
+                nc.sync.dma_start(out=freqs_sb[:], in_=freqs_rows)
+
+        identity = keep.tile([P, P], F32)
+        make_identity(nc, identity[:])
+        sign = keep.tile([P, 2], BF16)
+        nc.vector.memset(sign[:, 0:1], -1.0)
+        nc.vector.memset(sign[:, 1:2], 1.0)
+
+        w_grouped = keep.tile([P, 3 * W * PACK], BF16, align_bytes=64)
+        w_codes = keep.tile([P, 3 * W], U32, align_bytes=64)
+        w_scales = keep.tile([P, 3 * W], U8, align_bytes=64)
+        features_onto_partitions(nc, banks, identity[:], w_sb[:].bitcast(F32), w_grouped[:], 3)
+        for lo, hi in ((0, 2 * W), (2 * W, 3 * W)):
+            nc.vector.quantize_mx(
+                out=w_codes[:, lo:hi].bitcast(FP8X4),
+                scales=w_scales[:, lo:hi],
+                in_=w_grouped[:, lo * PACK : hi * PACK],
+            )
+
+        def quantise_round(r):
+            part = x_sb[r * ROUND // LOAD]
+            first = (r * ROUND) % LOAD
+            words = part[:].bitcast(F32)[:, first * D // 2 : (first + ROUND) * D // 2]
+            grouped = stage.tile([P, ROUND * P * PACK], BF16, align_bytes=64, name="grouped")
+            codes = stage.tile([P, ROUND * P], U32, align_bytes=64, name="codes")
+            scales = stage.tile([P, ROUND * P], U8, align_bytes=64, name="scales")
+            features_onto_partitions(nc, banks, identity[:], words, grouped[:], ROUND)
+            nc.vector.quantize_mx(out=codes[:].bitcast(FP8X4), scales=scales[:], in_=grouped[:])
+            return codes, scales
+
+        def rotary_factors(first_tile):
+            pairs = STORE * HD // 2
+            cos_sin = freqs_sb[:, first_tile * HD : (first_tile + STORE) * HD].rearrange(
+                "p (n c) -> p n c", c=2
+            )
+            signed_sin = stage.tile([P, pairs, 2], BF16, name="signed_sin")
+            nc.vector.tensor_tensor(
+                out=signed_sin[:],
+                in0=cos_sin[:, :, 1:2].to_broadcast([P, pairs, 2]),
+                in1=sign[:].unsqueeze(1).to_broadcast([P, pairs, 2]),
+                op=MULT,
+            )
+            factor = stage.tile([P, pairs, 2], F32, name="factor")
+            nc.vector.tensor_tensor(
+                out=factor[:],
+                in0=cos_sin[:, :, 0:1].to_broadcast([P, pairs, 2]),
+                in1=signed_sin[:],
+                op=ADD,
+            )
+            return factor[:].rearrange("p (t j) c -> p t (j c)", t=STORE)
+
+        ready = quantise_round(0)
+        for r in range(ROUNDS):
+            codes, scales = ready
+            local = (r * ROUND) % STORE
+            if local == 0:
+                factor = rotary_factors(r * ROUND)
+                result = results.tile([P, 3 * HEADS, STORE, HD], F32, name="result")
+            if r + 1 < ROUNDS:
+                ready = quantise_round(r + 1)
+
+            qk = []
+            for pair in range(ROUND // BANK_TILES):
+                qk_bank = qk_banks.tile([P, BANK_TILES, 2 * W], F32, name="qk_bank")
+                qk.append(qk_bank)
+            v_bank = v_banks.tile([P, ROUND, W], F32, name="v_bank")
+            for t in range(ROUND):
+                nc.tensor.matmul_mx(
+                    out=qk[t // BANK_TILES][:, t % BANK_TILES, :],
+                    lhsT=codes[:, t * P : (t + 1) * P].bitcast(FP8X4),
+                    lhsT_scale=scales[:, t * P : (t + 1) * P],
+                    rhs=w_codes[:, 0 : 2 * W].bitcast(FP8X4),
+                    rhs_scale=w_scales[:, 0 : 2 * W],
+                    start=True,
+                    stop=True,
+                )
+            for t in range(ROUND):
+                nc.tensor.matmul_mx(
+                    out=v_bank[:, t, :],
+                    lhsT=codes[:, t * P : (t + 1) * P].bitcast(FP8X4),
+                    lhsT_scale=scales[:, t * P : (t + 1) * P],
+                    rhs=w_codes[:, 2 * W : 3 * W].bitcast(FP8X4),
+                    rhs_scale=w_scales[:, 2 * W : 3 * W],
+                    start=True,
+                    stop=True,
+                )
+
+            for pair in range(ROUND // BANK_TILES):
+                t0 = local + pair * BANK_TILES
+                nc.vector.tensor_tensor(
+                    out=result[:, 0 : 2 * HEADS, t0 : t0 + BANK_TILES, :].rearrange("p a t d -> p t a d"),
+                    in0=qk[pair][:].rearrange("p t (a d) -> p t a d", d=HD),
+                    in1=factor[:, t0 : t0 + BANK_TILES, :]
+                    .unsqueeze(2)
+                    .to_broadcast([P, BANK_TILES, 2 * HEADS, HD]),
+                    op=MULT,
+                )
+            nc.scalar.copy(
+                out=result[:, 2 * HEADS : 3 * HEADS, local : local + ROUND, :].rearrange("p h t d -> p t h d"),
+                in_=v_bank[:].rearrange("p t (h d) -> p t h d", d=HD),
+            )
+
+            if local + ROUND == STORE:
+                first_tile = (r + 1) * ROUND - STORE
+                for i in range(3):
+                    nc.sync.dma_start(
+                        out=out_rows[i][:, :, first_tile : first_tile + STORE, :],
+                        in_=result[:, i * HEADS : (i + 1) * HEADS, :, :],
+                    )

@@ -56,23 +56,45 @@ def tile_attention_pa_t_kernel(tc, x, freqs, wq, wk, wv, out_0, out_1, out_2):
     ) as banks, tc.psum_pool(name="qk_banks", bufs=4) as qk_banks, tc.psum_pool(
         name="v_banks", bufs=2
     ) as v_banks:
+        freqs_sb = keep.tile([P, TILES * HD], BF16)
+        nc.sync.dma_start(out=freqs_sb[:], in_=freqs_rows)
         w_sb = keep.tile([P, 3 * D], BF16)
         for i, w in enumerate((wq, wk, wv)):
             nc.sync.dma_start(out=w_sb[:, i * D : (i + 1) * D], in_=w)
         x_sb = []
-        freqs_sb = keep.tile([P, TILES * HD], BF16)
         for c in range(TILES // LOAD):
             x_part = keep.tile([P, LOAD * D], BF16, name="x%d" % c)
-            nc.sync.dma_start(out=x_part[:], in_=x_rows[:, c * LOAD * D : (c + 1) * LOAD * D])
+            step = ROUND * D if c == 0 else LOAD * D
+            for lo in range(0, LOAD * D, step):
+                nc.sync.dma_start(
+                    out=x_part[:, lo : lo + step],
+                    in_=x_rows[:, c * LOAD * D + lo : c * LOAD * D + lo + step],
+                )
             x_sb.append(x_part)
-            if c == 0:
-                nc.sync.dma_start(out=freqs_sb[:], in_=freqs_rows)
 
         identity = keep.tile([P, P], F32)
         make_identity(nc, identity[:])
         sign = keep.tile([P, 2], BF16)
         nc.vector.memset(sign[:, 0:1], -1.0)
         nc.vector.memset(sign[:, 1:2], 1.0)
+
+        pairs = TILES * HD // 2
+        cos_sin = freqs_sb[:].rearrange("p (n c) -> p n c", c=2)
+        signed_sin = keep.tile([P, pairs, 2], BF16)
+        nc.vector.tensor_tensor(
+            out=signed_sin[:],
+            in0=cos_sin[:, :, 1:2].to_broadcast([P, pairs, 2]),
+            in1=sign[:].unsqueeze(1).to_broadcast([P, pairs, 2]),
+            op=MULT,
+        )
+        factor_pairs = keep.tile([P, pairs, 2], F32)
+        nc.vector.tensor_tensor(
+            out=factor_pairs[:],
+            in0=cos_sin[:, :, 0:1].to_broadcast([P, pairs, 2]),
+            in1=signed_sin[:],
+            op=ADD,
+        )
+        factor = factor_pairs[:].rearrange("p (t j) c -> p t (j c)", t=TILES)
 
         w_grouped = keep.tile([P, 3 * W * PACK], BF16, align_bytes=64)
         w_codes = keep.tile([P, 3 * W], U32, align_bytes=64)
@@ -96,33 +118,11 @@ def tile_attention_pa_t_kernel(tc, x, freqs, wq, wk, wv, out_0, out_1, out_2):
             nc.vector.quantize_mx(out=codes[:].bitcast(FP8X4), scales=scales[:], in_=grouped[:])
             return codes, scales
 
-        def rotary_factors(first_tile):
-            pairs = STORE * HD // 2
-            cos_sin = freqs_sb[:, first_tile * HD : (first_tile + STORE) * HD].rearrange(
-                "p (n c) -> p n c", c=2
-            )
-            signed_sin = stage.tile([P, pairs, 2], BF16, name="signed_sin")
-            nc.vector.tensor_tensor(
-                out=signed_sin[:],
-                in0=cos_sin[:, :, 1:2].to_broadcast([P, pairs, 2]),
-                in1=sign[:].unsqueeze(1).to_broadcast([P, pairs, 2]),
-                op=MULT,
-            )
-            factor = stage.tile([P, pairs, 2], F32, name="factor")
-            nc.vector.tensor_tensor(
-                out=factor[:],
-                in0=cos_sin[:, :, 0:1].to_broadcast([P, pairs, 2]),
-                in1=signed_sin[:],
-                op=ADD,
-            )
-            return factor[:].rearrange("p (t j) c -> p t (j c)", t=STORE)
-
         ready = quantise_round(0)
         for r in range(ROUNDS):
             codes, scales = ready
             local = (r * ROUND) % STORE
             if local == 0:
-                factor = rotary_factors(r * ROUND)
                 result = results.tile([P, 3 * HEADS, STORE, HD], F32, name="result")
             if r + 1 < ROUNDS:
                 ready = quantise_round(r + 1)
@@ -155,10 +155,11 @@ def tile_attention_pa_t_kernel(tc, x, freqs, wq, wk, wv, out_0, out_1, out_2):
 
             for pair in range(ROUND // BANK_TILES):
                 t0 = local + pair * BANK_TILES
+                tile0 = r * ROUND + pair * BANK_TILES
                 nc.vector.tensor_tensor(
                     out=result[:, 0 : 2 * HEADS, t0 : t0 + BANK_TILES, :].rearrange("p a t d -> p t a d"),
                     in0=qk[pair][:].rearrange("p t (a d) -> p t a d", d=HD),
-                    in1=factor[:, t0 : t0 + BANK_TILES, :]
+                    in1=factor[:, tile0 : tile0 + BANK_TILES, :]
                     .unsqueeze(2)
                     .to_broadcast([P, BANK_TILES, 2 * HEADS, HD]),
                     op=MULT,

@@ -22,7 +22,7 @@ TILES = S // P
 BANK_TILES = 2
 ROUND = 4
 LOAD = 8
-STORE = 16
+STORE = 24
 ROUNDS = TILES // ROUND
 
 FLOPS = 2 * S * D * 3 * W
@@ -51,7 +51,7 @@ def tile_attention_pa_t_kernel(tc, x, freqs, wq, wk, wv, out_0, out_1, out_2):
 
     with tc.manual_schedule(), tc.tile_pool(name="keep", bufs=1) as keep, tc.tile_pool(
         name="stage", bufs=3
-    ) as stage, tc.tile_pool(name="results", bufs=TILES // STORE) as results, tc.psum_pool(
+    ) as stage, tc.tile_pool(name="results", bufs=-(-TILES // STORE)) as results, tc.psum_pool(
         name="banks", bufs=2
     ) as banks, tc.psum_pool(name="qk_banks", bufs=4) as qk_banks, tc.psum_pool(
         name="v_banks", bufs=2
@@ -169,10 +169,11 @@ def tile_attention_pa_t_kernel(tc, x, freqs, wq, wk, wv, out_0, out_1, out_2):
                 in_=v_bank[:].rearrange("p t (h d) -> p t h d", d=HD),
             )
 
-            if local + ROUND == STORE:
-                first_tile = (r + 1) * ROUND - STORE
+            first_tile = r * ROUND - local
+            count = min(STORE, TILES - first_tile)
+            if local + ROUND == count:
                 for i in range(3):
                     nc.sync.dma_start(
-                        out=out_rows[i][:, :, first_tile : first_tile + STORE, :],
-                        in_=result[:, i * HEADS : (i + 1) * HEADS, :, :],
+                        out=out_rows[i][:, :, first_tile : first_tile + count, :],
+                        in_=result[:, i * HEADS : (i + 1) * HEADS, 0:count, :],
                     )

@@ -22,7 +22,7 @@ TILES = S // P
 BANK_TILES = 2
 ROUND = 4
 LOAD = 8
-STORE = 24
+STORE = 16
 ROUNDS = TILES // ROUND
 
 FLOPS = 2 * S * D * 3 * W
@@ -51,7 +51,7 @@ def tile_attention_pa_t_kernel(tc, x, freqs, wq, wk, wv, out_0, out_1, out_2):
 
     with tc.manual_schedule(), tc.tile_pool(name="keep", bufs=1) as keep, tc.tile_pool(
         name="stage", bufs=3
-    ) as stage, tc.tile_pool(name="results", bufs=-(-TILES // STORE)) as results, tc.psum_pool(
+    ) as stage, tc.tile_pool(name="results", bufs=TILES // STORE) as results, tc.psum_pool(
         name="banks", bufs=2
     ) as banks, tc.psum_pool(name="qk_banks", bufs=4) as qk_banks, tc.psum_pool(
         name="v_banks", bufs=2
@@ -169,11 +169,12 @@ def tile_attention_pa_t_kernel(tc, x, freqs, wq, wk, wv, out_0, out_1, out_2):
                 in_=v_bank[:].rearrange("p t (h d) -> p t h d", d=HD),
             )
 
-            first_tile = r * ROUND - local
-            count = min(STORE, TILES - first_tile)
-            if local + ROUND == count:
+            cut = STORE // 2 if (r + 1) * ROUND > TILES - STORE else STORE
+            done = local + ROUND
+            if done % cut == 0:
+                first_tile = (r + 1) * ROUND - cut
                 for i in range(3):
                     nc.sync.dma_start(
-                        out=out_rows[i][:, :, first_tile : first_tile + count, :],
-                        in_=result[:, i * HEADS : (i + 1) * HEADS, 0:count, :],
+                        out=out_rows[i][:, :, first_tile : first_tile + cut, :],
+                        in_=result[:, i * HEADS : (i + 1) * HEADS, done - cut : done, :],
                     )

import concourse.mybir as mybir
from concourse.masks import make_identity

F32 = mybir.dt.float32
BF16 = mybir.dt.bfloat16
U32 = mybir.dt.uint32
U8 = mybir.dt.uint8
FP8X4 = mybir.dt.float8_e4m3fn_x4
MULT = mybir.AluOpType.mult
ADD = mybir.AluOpType.add

P = 128
S = 8192
D = 512
HEADS = 4
HD = 32
W = HEADS * HD
PACK = 4
HALVES = 2

TILES = S // P
BANK_TILES = 2
ROUND = 4
LOAD = 8
STORE = 16
ROUNDS = TILES // ROUND

FLOPS = 2 * S * D * 3 * W


def features_onto_partitions(nc, banks, identity, words, grouped, tiles):
    grouped_words = grouped.bitcast(F32).rearrange("p (t r u) -> p t r u", r=P, u=HALVES)
    for first in range(0, tiles, BANK_TILES):
        count = min(BANK_TILES, tiles - first)
        bank = banks.tile([P, BANK_TILES, HALVES, P], F32, name="transposed")
        for t in range(count):
            for u in range(HALVES):
                column = ((first + t) * HALVES + u) * P
                nc.tensor.transpose(bank[:, t, u, :], words[:, column : column + P], identity)
        nc.scalar.copy(
            out=grouped_words[:, first : first + count],
            in_=bank[:, 0:count].rearrange("p t u r -> p t r u"),
        )


def tile_attention_pa_t_kernel(tc, x, freqs, wq, wk, wv, out_0, out_1, out_2):
    nc = tc.nc
    x_rows = x.rearrange("(p t) k -> p (t k)", t=TILES)
    freqs_rows = freqs.rearrange("(p t) j c -> p (t j c)", t=TILES)
    out_rows = [o.rearrange("h (p t) d -> p h t d", t=TILES) for o in (out_0, out_1, out_2)]

    with tc.manual_schedule(), tc.tile_pool(name="keep", bufs=1) as keep, tc.tile_pool(
        name="stage", bufs=3
    ) as stage, tc.tile_pool(name="results", bufs=TILES // STORE) as results, tc.psum_pool(
        name="banks", bufs=2
    ) as banks, tc.psum_pool(name="qk_banks", bufs=4) as qk_banks, tc.psum_pool(
        name="v_banks", bufs=2
    ) as v_banks:
        freqs_sb = keep.tile([P, TILES * HD], BF16)
        nc.sync.dma_start(out=freqs_sb[:], in_=freqs_rows)
        w_sb = keep.tile([P, 3 * D], BF16)
        for i, w in enumerate((wq, wk, wv)):
            nc.sync.dma_start(out=w_sb[:, i * D : (i + 1) * D], in_=w)
        x_sb = []
        for c in range(TILES // LOAD):
            x_part = keep.tile([P, LOAD * D], BF16, name="x%d" % c)
            step = ROUND * D if c == 0 else LOAD * D
            for lo in range(0, LOAD * D, step):
                nc.sync.dma_start(
                    out=x_part[:, lo : lo + step],
                    in_=x_rows[:, c * LOAD * D + lo : c * LOAD * D + lo + step],
                )
            x_sb.append(x_part)

        identity = keep.tile([P, P], F32)
        make_identity(nc, identity[:])
        sign = keep.tile([P, 2], BF16)
        nc.vector.memset(sign[:, 0:1], -1.0)
        nc.vector.memset(sign[:, 1:2], 1.0)

        pairs = TILES * HD // 2
        cos_sin = freqs_sb[:].rearrange("p (n c) -> p n c", c=2)
        signed_sin = keep.tile([P, pairs, 2], BF16)
        nc.vector.tensor_tensor(
            out=signed_sin[:],
            in0=cos_sin[:, :, 1:2].to_broadcast([P, pairs, 2]),
            in1=sign[:].unsqueeze(1).to_broadcast([P, pairs, 2]),
            op=MULT,
        )
        factor_pairs = keep.tile([P, pairs, 2], F32)
        nc.vector.tensor_tensor(
            out=factor_pairs[:],
            in0=cos_sin[:, :, 0:1].to_broadcast([P, pairs, 2]),
            in1=signed_sin[:],
            op=ADD,
        )
        factor = factor_pairs[:].rearrange("p (t j) c -> p t (j c)", t=TILES)

        w_grouped = keep.tile([P, 3 * W * PACK], BF16, align_bytes=64)
        w_codes = keep.tile([P, 3 * W], U32, align_bytes=64)
        w_scales = keep.tile([P, 3 * W], U8, align_bytes=64)
        features_onto_partitions(nc, banks, identity[:], w_sb[:].bitcast(F32), w_grouped[:], 3)
        for lo, hi in ((0, 2 * W), (2 * W, 3 * W)):
            nc.vector.quantize_mx(
                out=w_codes[:, lo:hi].bitcast(FP8X4),
                scales=w_scales[:, lo:hi],
                in_=w_grouped[:, lo * PACK : hi * PACK],
            )

        def quantise_round(r):
            part = x_sb[r * ROUND // LOAD]
            first = (r * ROUND) % LOAD
            words = part[:].bitcast(F32)[:, first * D // 2 : (first + ROUND) * D // 2]
            grouped = stage.tile([P, ROUND * P * PACK], BF16, align_bytes=64, name="grouped")
            codes = stage.tile([P, ROUND * P], U32, align_bytes=64, name="codes")
            scales = stage.tile([P, ROUND * P], U8, align_bytes=64, name="scales")
            features_onto_partitions(nc, banks, identity[:], words, grouped[:], ROUND)
            nc.vector.quantize_mx(out=codes[:].bitcast(FP8X4), scales=scales[:], in_=grouped[:])
            return codes, scales

        ready = quantise_round(0)
        for r in range(ROUNDS):
            codes, scales = ready
            local = (r * ROUND) % STORE
            if local == 0:
                result = results.tile([P, 3 * HEADS, STORE, HD], F32, name="result")
            if r + 1 < ROUNDS:
                ready = quantise_round(r + 1)

            qk = []
            for pair in range(ROUND // BANK_TILES):
                qk_bank = qk_banks.tile([P, BANK_TILES, 2 * W], F32, name="qk_bank")
                qk.append(qk_bank)
            v_bank = v_banks.tile([P, ROUND, W], F32, name="v_bank")
            for t in range(ROUND):
                nc.tensor.matmul_mx(
                    out=qk[t // BANK_TILES][:, t % BANK_TILES, :],
                    lhsT=codes[:, t * P : (t + 1) * P].bitcast(FP8X4),
                    lhsT_scale=scales[:, t * P : (t + 1) * P],
                    rhs=w_codes[:, 0 : 2 * W].bitcast(FP8X4),
                    rhs_scale=w_scales[:, 0 : 2 * W],
                    start=True,
                    stop=True,
                )
            for t in range(ROUND):
                nc.tensor.matmul_mx(
                    out=v_bank[:, t, :],
                    lhsT=codes[:, t * P : (t + 1) * P].bitcast(FP8X4),
                    lhsT_scale=scales[:, t * P : (t + 1) * P],
                    rhs=w_codes[:, 2 * W : 3 * W].bitcast(FP8X4),
                    rhs_scale=w_scales[:, 2 * W : 3 * W],
                    start=True,
                    stop=True,
                )

            for pair in range(ROUND // BANK_TILES):
                t0 = local + pair * BANK_TILES
                tile0 = r * ROUND + pair * BANK_TILES
                nc.vector.tensor_tensor(
                    out=result[:, 0 : 2 * HEADS, t0 : t0 + BANK_TILES, :].rearrange("p a t d -> p t a d"),
                    in0=qk[pair][:].rearrange("p t (a d) -> p t a d", d=HD),
                    in1=factor[:, tile0 : tile0 + BANK_TILES, :]
                    .unsqueeze(2)
                    .to_broadcast([P, BANK_TILES, 2 * HEADS, HD]),
                    op=MULT,
                )
            nc.scalar.copy(
                out=result[:, 2 * HEADS : 3 * HEADS, local : local + ROUND, :].rearrange("p h t d -> p t h d"),
                in_=v_bank[:].rearrange("p t (h d) -> p t h d", d=HD),
            )

            cut = STORE // 2 if (r + 1) * ROUND > TILES - STORE else STORE
            done = local + ROUND
            if done % cut == 0:
                first_tile = (r + 1) * ROUND - cut
                for i in range(3):
                    nc.sync.dma_start(
                        out=out_rows[i][:, :, first_tile : first_tile + cut, :],
                        in_=result[:, i * HEADS : (i + 1) * HEADS, done - cut : done, :],
                    )
